import numpy as np
import ml_dtypes


def mxq(x, axis, fmt="e4m3"):
    dtype, down = {"e4m3": (ml_dtypes.float8_e4m3fn, 7), "e5m2": (ml_dtypes.float8_e5m2, 14)}[fmt]
    v = np.moveaxis(np.asarray(x, np.float32).astype(ml_dtypes.bfloat16).astype(np.float64), axis, -1)
    blocks = v.reshape(v.shape[:-1] + (-1, 32))
    amax = np.abs(blocks).max(-1, keepdims=True)
    byte = np.maximum(np.where(amax > 0, np.frexp(amax)[1] - 1 + 127, 0) - down, 1)
    scale = np.exp2(byte - 127.0)
    codes = (blocks / scale).astype(np.float32).astype(dtype).astype(np.float64)
    return np.moveaxis((codes * scale).reshape(v.shape), -1, axis)


WIDE = False


def mx_kscale(k):
    if not WIDE:
        return np.ones(k)
    levels = np.array([10, -10, 5, -5, 0])
    a = np.random.permutation(np.resize(levels, k // 512 * 4)).reshape(k // 512, 4)
    idx = np.arange(k)
    return np.exp2(a[idx // 512, idx % 128 // 32])


BF16 = ml_dtypes.bfloat16


def bf(x):
    return np.asarray(x, np.float32).astype(BF16)


def f64(x):
    return np.asarray(x).astype(np.float64)


E2M1 = np.array([0.0, 0.5, 1.0, 1.5, 2.0, 3.0, 4.0, 6.0, -0.0, -0.5, -1.0, -1.5, -2.0, -3.0, -4.0, -6.0])


def pack_weight(w, fmt):
    k, n = w.shape
    w = f64(bf(w)).reshape(k // 32, 32, n)
    amax = np.abs(w).max(1)
    if fmt == "e4m3":
        byte = np.frexp(amax)[1] - 1 + 127 - 7
    else:
        mant, ex = np.frexp(amax / 6.0)
        byte = np.where(mant > 0.5, ex, ex - 1) + 127
    byte = np.clip(np.where(amax > 0, byte, 1), 1, 254)
    scaled = (w * np.exp2(127.0 - byte)[:, None, :]).reshape(k, n).astype(np.float32)
    by_word = np.ascontiguousarray(scaled.reshape(k // 512, 128, 4, n).transpose(0, 1, 3, 2))
    if fmt == "e4m3":
        words = by_word.astype(ml_dtypes.float8_e4m3fn).view(np.uint8)
    else:
        c = by_word.astype(ml_dtypes.float4_e2m1fn).view(np.uint8) & 0xF
        words = c[..., 0::2] | (c[..., 1::2] << 4)
    return np.ascontiguousarray(words), np.ascontiguousarray(byte.astype(np.uint8).reshape(k // 512, 16, n))


def unpack_weight(words, scales, fmt):
    g, p, n, _ = words.shape
    if fmt == "e4m3":
        vals = np.ascontiguousarray(words).view(ml_dtypes.float8_e4m3fn).astype(np.float64)
    else:
        nib = np.empty((g, p, n, 4), np.uint8)
        nib[..., 0::2] = words & 0xF
        nib[..., 1::2] = words >> 4
        vals = E2M1[nib]
    vals = vals * np.repeat(np.exp2(scales.astype(np.float64) - 127.0), 8, axis=1)[..., None]
    return vals.transpose(0, 1, 3, 2).reshape(g * 512, n)

def pack4(w):
    words, scales = pack_weight(w, "e2m1")
    return words.reshape(words.shape[0], 128, -1), scales


def unpack4(words, scales):
    return unpack_weight(words.reshape(words.shape[0], 128, -1, 2), scales, "e2m1")


B, S, HID, NH, NOPE, ROPE, VD, KV_RANK, SW, QB = 1, 256, 512, 8, 64, 128, 128, 512, 384, 128
QK = NOPE + ROPE


def rotate_half(x):
    h = x.shape[-1] // 2
    return np.concatenate([-x[..., h:], x[..., :h]], axis=-1)


def rope_tables():
    pos = np.arange(S, dtype=np.float64)
    inv = 1.0 / (10000.0 ** (np.arange(0, ROPE, 2, dtype=np.float64) / ROPE))
    ang = pos[:, None] * inv[None, :]
    ang = np.concatenate([ang, ang], axis=-1)
    return bf(np.broadcast_to(np.cos(ang)[None], (B, S, ROPE))), bf(np.broadcast_to(np.sin(ang)[None], (B, S, ROPE)))


def setup_inputs():
    s = mx_kscale(HID)
    cos, sin = rope_tables()
    hidden_states = bf(np.random.standard_normal((B, S, HID)) * s)
    Wq_words, Wq_scales = pack4(np.random.standard_normal((HID, NH * QK)) * 2.0 / np.sqrt(HID) / s[:, None])
    bq = bf(np.random.standard_normal(NH * QK) * 0.2)
    return {"hidden_states": hidden_states, "cos": cos, "sin": sin,
            "Wq_words": Wq_words, "Wq_scales": Wq_scales,
            "bq": bq}


def reference(hidden_states, cos, sin, Wq_words, Wq_scales, bq):
    q = ((mxq(f64(hidden_states), 2, "e4m3") @ unpack4(Wq_words, Wq_scales)) + f64(bq)).reshape(B, S, NH, QK).transpose(0, 2, 1, 3)
    q_nope, q_rope = q[..., :NOPE], q[..., NOPE:]
    c, si = f64(cos)[:, None], f64(sin)[:, None]
    q_rope = q_rope * c + rotate_half(q_rope) * si
    return np.concatenate([q_nope, q_rope], axis=-1)

@@ -1,0 +1,133 @@
+from contextlib import ExitStack
+
+import concourse.mybir as mybir
+from concourse.masks import make_identity
+
+F32 = mybir.dt.float32
+BF16 = mybir.dt.bfloat16
+I32 = mybir.dt.int32
+U8 = mybir.dt.uint8
+U32 = mybir.dt.uint32
+FP8X4 = mybir.dt.float8_e4m3fn_x4
+FP4X4 = mybir.dt.float4_e2m1fn_x4
+ADD = mybir.AluOpType.add
+MULT = mybir.AluOpType.mult
+
+P = 128
+SEQ = 256
+HID = 512
+HEADS = 8
+NOPE = 64
+ROPE = 128
+HALF = ROPE // 2
+HEAD = NOPE + ROPE
+N_OUT = HEADS * HEAD
+T = SEQ // P
+PAIR = 2 * HEAD
+
+FLOPS = 2 * SEQ * HID * N_OUT
+
+
+def tile_gptossmlaattention_pb_s_kernel(
+    tc, hidden_states, cos, sin, Wq_words, Wq_scales, bq, out
+):
+    nc = tc.nc
+    with ExitStack() as ctx:
+        keep = ctx.enter_context(tc.tile_pool(name="keep", bufs=1))
+        work = ctx.enter_context(tc.tile_pool(name="work", bufs=2))
+        psum = ctx.enter_context(tc.psum_pool(name="psum", bufs=8))
+
+        x_sb = keep.tile([P, T, HID], BF16)
+        nc.sync.dma_start(
+            out=x_sb[:], in_=hidden_states.rearrange("b (p t) k -> p (b t) k", t=T)
+        )
+        w_scales = keep.tile([P, N_OUT], U8, align_bytes=64)
+        nc.vector.memset(w_scales[:].bitcast(I32), 0)
+        for quad in range(4):
+            nc.sync.dma_start(
+                out=w_scales[32 * quad : 32 * quad + 4, :].bitcast(I32),
+                in_=Wq_scales[0, 4 * quad : 4 * quad + 4, :].bitcast(I32),
+            )
+        w_words = keep.tile([P, 2 * N_OUT], U8, align_bytes=64)
+        nc.sync.dma_start(out=w_words[:].bitcast(I32), in_=Wq_words[0].bitcast(I32))
+
+        bias_all = keep.tile([P, N_OUT], BF16)
+        nc.scalar.dma_start(out=bias_all[:], in_=bq.partition_broadcast(P))
+        cos_sb = keep.tile([P, T, ROPE], BF16)
+        nc.scalar.dma_start(out=cos_sb[:], in_=cos.rearrange("b (p t) j -> p (b t) j", t=T))
+        sin_sb = keep.tile([P, T, ROPE], BF16)
+        nc.scalar.dma_start(out=sin_sb[:], in_=sin.rearrange("b (p t) j -> p (b t) j", t=T))
+
+        ident = keep.tile([P, P], F32)
+        make_identity(nc, ident[:])
+
+        nc.scalar.mul(out=sin_sb[:, :, 0:HALF], in_=sin_sb[:, :, 0:HALF], mul=-1.0)
+
+        x_words = x_sb[:].bitcast(F32)
+        xt_ps = psum.tile([P, 2, SEQ], F32, tag="bank")
+        for t in range(T):
+            for u in range(2):
+                nc.tensor.transpose(
+                    xt_ps[:, u, t * P : (t + 1) * P], x_words[:, t, u : HID // 2 : 2], ident[:]
+                )
+        x_grouped = keep.tile([P, 4 * SEQ], BF16, align_bytes=64)
+        nc.vector.tensor_copy(
+            out=x_grouped[:].bitcast(F32).rearrange("p (c u) -> p c u", u=2),
+            in_=xt_ps[:].rearrange("p u c -> p c u"),
+        )
+        x_codes = keep.tile([P, SEQ], U32, align_bytes=64)
+        x_scales = keep.tile([P, SEQ], U8, align_bytes=64)
+        nc.vector.quantize_mx(
+            out=x_codes[:].bitcast(FP8X4), scales=x_scales[:], in_=x_grouped[:]
+        )
+
+        o_sb = keep.tile([P, HEADS, T, HEAD], F32)
+        out_v = out.rearrange("b h (p t) d -> p (b h) (t d)", t=T)
+        for g in range(HEADS // 2):
+            heads = slice(2 * g, 2 * g + 2)
+            first = PAIR * g
+            for t in range(T):
+                rows = slice(t * P, (t + 1) * P)
+                q_ps = psum.tile([P, PAIR], F32, tag="bank")
+                for lo, hi in ((0, 256), (256, PAIR)):
+                    nc.tensor.matmul_mx(
+                        out=q_ps[:, lo:hi],
+                        lhsT=x_codes[:, rows].bitcast(FP8X4),
+                        lhsT_scale=x_scales[:, rows],
+                        rhs=w_words[:, 2 * (first + lo) : 2 * (first + hi)].bitcast(FP4X4),
+                        rhs_scale=w_scales[:, first + lo : first + hi],
+                        start=True,
+                        stop=True,
+                    )
+                nc.vector.tensor_tensor(
+                    out=o_sb[:, heads, t, :],
+                    in0=q_ps[:].rearrange("p (h d) -> p h d", d=HEAD),
+                    in1=bias_all[:, first : first + PAIR].rearrange("p (h d) -> p h d", d=HEAD),
+                    op=ADD,
+                )
+            lower = o_sb[:, heads, :, NOPE : NOPE + HALF]
+            upper = o_sb[:, heads, :, NOPE + HALF : HEAD]
+            both = o_sb[:, heads, :, NOPE:HEAD]
+            turned = work.tile([P, 2, T, ROPE], F32)
+            nc.vector.tensor_tensor(
+                out=turned[:, :, :, 0:HALF],
+                in0=upper,
+                in1=sin_sb[:, :, 0:HALF].unsqueeze(1).to_broadcast([P, 2, T, HALF]),
+                op=MULT,
+            )
+            nc.vector.tensor_tensor(
+                out=turned[:, :, :, HALF:ROPE],
+                in0=lower,
+                in1=sin_sb[:, :, HALF:ROPE].unsqueeze(1).to_broadcast([P, 2, T, HALF]),
+                op=MULT,
+            )
+            nc.vector.tensor_tensor(
+                out=both,
+                in0=both,
+                in1=cos_sb[:].unsqueeze(1).to_broadcast([P, 2, T, ROPE]),
+                op=MULT,
+            )
+            nc.vector.tensor_tensor(out=both, in0=both, in1=turned[:], op=ADD)
+            nc.sync.dma_start(
+                out=out_v[:, heads, :], in_=o_sb[:, heads, :, :].rearrange("p h t d -> p h (t d)")
+            )

@@ -12,6 +12,7 @@ FP8X4 = mybir.dt.float8_e4m3fn_x4
 FP4X4 = mybir.dt.float4_e2m1fn_x4
 ADD = mybir.AluOpType.add
 MULT = mybir.AluOpType.mult
+IDENTITY = mybir.ActivationFunctionType.Identity
 
 P = 128
 SEQ = 256
@@ -23,7 +24,7 @@ HALF = ROPE // 2
 HEAD = NOPE + ROPE
 N_OUT = HEADS * HEAD
 T = SEQ // P
-PAIR = 2 * HEAD
+PAIRS = HEADS // 2
 
 FLOPS = 2 * SEQ * HID * N_OUT
 
@@ -34,15 +35,30 @@ def tile_gptossmlaattention_pb_s_kernel(
     nc = tc.nc
     with ExitStack() as ctx:
         keep = ctx.enter_context(tc.tile_pool(name="keep", bufs=1))
-        work = ctx.enter_context(tc.tile_pool(name="work", bufs=2))
-        psum = ctx.enter_context(tc.psum_pool(name="psum", bufs=8))
+        per_head = ctx.enter_context(tc.tile_pool(name="per_head", bufs=HEADS))
+        q_banks = ctx.enter_context(tc.psum_pool(name="q_banks", bufs=4))
+        o_banks = ctx.enter_context(tc.psum_pool(name="o_banks", bufs=4))
+        ctx.enter_context(tc.manual_schedule())
 
+        bias_rows = keep.tile([P, P], BF16)
+        nc.vector.memset(bias_rows[:], 0.0)
+        w_scales = keep.tile([P, N_OUT], U8, align_bytes=64)
+        nc.vector.memset(w_scales[:].bitcast(I32), 0)
+        warm = keep.tile([P, 1], F32)
+        nc.vector.memset(warm[:], 0.0)
+        nc.scalar.activation(out=warm[:], in_=warm[:], func=IDENTITY)
+
+        nc.scalar.dma_start(
+            out=bias_rows[0:HEADS, :], in_=bq.rearrange("(h d) -> h d", d=HEAD)[:, NOPE:HEAD]
+        )
+        nc.scalar.dma_start(
+            out=bias_rows[HEADS : HEADS + PAIRS, :].rearrange("m (e j) -> m e j", e=2),
+            in_=bq.rearrange("(m e d) -> m e d", e=2, d=HEAD)[:, :, 0:NOPE],
+        )
         x_sb = keep.tile([P, T, HID], BF16)
         nc.sync.dma_start(
             out=x_sb[:], in_=hidden_states.rearrange("b (p t) k -> p (b t) k", t=T)
         )
-        w_scales = keep.tile([P, N_OUT], U8, align_bytes=64)
-        nc.vector.memset(w_scales[:].bitcast(I32), 0)
         for quad in range(4):
             nc.sync.dma_start(
                 out=w_scales[32 * quad : 32 * quad + 4, :].bitcast(I32),
@@ -50,25 +66,25 @@ def tile_gptossmlaattention_pb_s_kernel(
             )
         w_words = keep.tile([P, 2 * N_OUT], U8, align_bytes=64)
         nc.sync.dma_start(out=w_words[:].bitcast(I32), in_=Wq_words[0].bitcast(I32))
-
-        bias_all = keep.tile([P, N_OUT], BF16)
-        nc.scalar.dma_start(out=bias_all[:], in_=bq.partition_broadcast(P))
         cos_sb = keep.tile([P, T, ROPE], BF16)
         nc.scalar.dma_start(out=cos_sb[:], in_=cos.rearrange("b (p t) j -> p (b t) j", t=T))
         sin_sb = keep.tile([P, T, ROPE], BF16)
         nc.scalar.dma_start(out=sin_sb[:], in_=sin.rearrange("b (p t) j -> p (b t) j", t=T))
 
-        ident = keep.tile([P, P], F32)
-        make_identity(nc, ident[:])
-
-        nc.scalar.mul(out=sin_sb[:, :, 0:HALF], in_=sin_sb[:, :, 0:HALF], mul=-1.0)
+        eye = keep.tile([P, HALF + P], F32)
+        make_identity(nc, eye[:, HALF : HALF + P])
+        ident = eye[:, HALF : HALF + P]
+        exchange = eye[:, 0:P]
+        ident_bf = keep.tile([P, P], BF16)
+        make_identity(nc, ident_bf[:])
+        nc.gpsimd.tensor_copy(out=eye[:, 0:HALF], in_=eye[:, P : P + HALF])
 
         x_words = x_sb[:].bitcast(F32)
-        xt_ps = psum.tile([P, 2, SEQ], F32, tag="bank")
+        xt_ps = o_banks.tile([P, 2, SEQ], F32, tag="o")
         for t in range(T):
             for u in range(2):
                 nc.tensor.transpose(
-                    xt_ps[:, u, t * P : (t + 1) * P], x_words[:, t, u : HID // 2 : 2], ident[:]
+                    xt_ps[:, u, t * P : (t + 1) * P], x_words[:, t, u : HID // 2 : 2], ident
                 )
         x_grouped = keep.tile([P, 4 * SEQ], BF16, align_bytes=64)
         nc.vector.tensor_copy(
@@ -80,54 +96,114 @@ def tile_gptossmlaattention_pb_s_kernel(
         nc.vector.quantize_mx(
             out=x_codes[:].bitcast(FP8X4), scales=x_scales[:], in_=x_grouped[:]
         )
+        nope_words = keep.tile([P, 2 * HEADS * NOPE], U8, align_bytes=64)
+        nc.vector.tensor_copy(
+            out=nope_words[:].bitcast(I32).rearrange("p (h w) -> p h w", h=HEADS),
+            in_=w_words[:].bitcast(I32).rearrange("p (h w) -> p h w", h=HEADS)[:, :, 0 : NOPE // 2],
+        )
+        nope_scales = keep.tile([P, HEADS * NOPE], U8, align_bytes=64)
+        nc.vector.tensor_copy(
+            out=nope_scales[:].bitcast(I32).rearrange("p (h w) -> p h w", h=HEADS),
+            in_=w_scales[:].bitcast(I32).rearrange("p (h w) -> p h w", h=HEADS)[:, :, 0 : NOPE // 4],
+        )
+
+        bias_ps = q_banks.tile([P, P], BF16, tag="q")
+        nc.tensor.transpose(bias_ps[:], bias_rows[:], ident_bf[:])
+        bias_t = keep.tile([P, HEADS + PAIRS], F32)
+        nc.scalar.copy(out=bias_t[:], in_=bias_ps[:, 0 : HEADS + PAIRS])
+        sin_x = keep.tile([P, T, ROPE], BF16)
+        nc.scalar.copy(out=sin_x[:, :, 0:HALF], in_=sin_sb[:, :, HALF:ROPE])
+        nc.scalar.mul(out=sin_x[:, :, HALF:ROPE], in_=sin_sb[:, :, 0:HALF], mul=-1.0)
+        tables_ps = o_banks.tile([P, 2, SEQ], BF16, tag="o")
+        for t in range(T):
+            nc.tensor.transpose(tables_ps[:, 0, t * P : (t + 1) * P], cos_sb[:, t, :], ident_bf[:])
+        for t in range(T):
+            nc.tensor.transpose(tables_ps[:, 1, t * P : (t + 1) * P], sin_x[:, t, :], ident_bf[:])
+        tables_t = keep.tile([P, 2, SEQ], BF16)
+        nc.scalar.copy(out=tables_t[:, 0, :], in_=tables_ps[:, 0, :])
+        nc.scalar.copy(out=tables_t[:, 1, :], in_=tables_ps[:, 1, :])
+        cos_t = tables_t[:, 0, :]
+        sin_t = tables_t[:, 1, :]
+
+        def passes(bank, words, scales, first, step):
+            for i in range(2):
+                lo = first + i * step
+                nc.tensor.matmul_mx(
+                    out=bank[:, i, :],
+                    lhsT=words[:, 2 * lo : 2 * (lo + P)].bitcast(FP4X4),
+                    lhsT_scale=scales[:, lo : lo + P],
+                    rhs=x_codes[:].bitcast(FP8X4),
+                    rhs_scale=x_scales[:],
+                    start=True,
+                    stop=True,
+                )
+
+        def rope_passes(m):
+            bank = q_banks.tile([P, 2, SEQ], F32, tag="q", name="rope_q")
+            passes(bank, w_words, w_scales, 2 * m * HEAD + NOPE, HEAD)
+            return bank
+
+        def nope_passes(b):
+            bank = o_banks.tile([P, 2, SEQ], F32, tag="o", name="nope_q")
+            passes(bank, nope_words, nope_scales, 2 * b * P, P)
+            return bank
+
+        rope_q = [rope_passes(0)]
+        nope_q = [nope_passes(b) for b in range(PAIRS // 2)]
+        rope_q.extend([rope_passes(m) for m in range(1, PAIRS)])
+
+        plain = keep.tile([P, PAIRS, SEQ], F32)
+        for m in range(PAIRS):
+            nc.scalar.activation(
+                out=plain[:, m, :],
+                in_=nope_q[m // 2][:, m % 2, :],
+                func=IDENTITY,
+                bias=bias_t[:, HEADS + m : HEADS + m + 1],
+            )
 
         o_sb = keep.tile([P, HEADS, T, HEAD], F32)
         out_v = out.rearrange("b h (p t) d -> p (b h) (t d)", t=T)
-        for g in range(HEADS // 2):
-            heads = slice(2 * g, 2 * g + 2)
-            first = PAIR * g
+
+        def rope_head(h):
+            q_t = rope_q[h // 2][:, h % 2, :]
+            straight = per_head.tile([P, SEQ], F32, name="straight")
+            nc.vector.scalar_tensor_tensor(
+                out=straight[:], in0=q_t, scalar=bias_t[:, h : h + 1], in1=cos_t, op0=ADD, op1=MULT
+            )
+            crossed = per_head.tile([P, SEQ], F32, name="crossed")
+            nc.vector.scalar_tensor_tensor(
+                out=crossed[:], in0=q_t, scalar=bias_t[:, h : h + 1], in1=sin_t, op0=ADD, op1=MULT
+            )
+            rope_ps = o_banks.tile([P, T, P], F32, tag="o", name="rope_ps")
             for t in range(T):
                 rows = slice(t * P, (t + 1) * P)
-                q_ps = psum.tile([P, PAIR], F32, tag="bank")
-                for lo, hi in ((0, 256), (256, PAIR)):
-                    nc.tensor.matmul_mx(
-                        out=q_ps[:, lo:hi],
-                        lhsT=x_codes[:, rows].bitcast(FP8X4),
-                        lhsT_scale=x_scales[:, rows],
-                        rhs=w_words[:, 2 * (first + lo) : 2 * (first + hi)].bitcast(FP4X4),
-                        rhs_scale=w_scales[:, first + lo : first + hi],
-                        start=True,
-                        stop=True,
-                    )
-                nc.vector.tensor_tensor(
-                    out=o_sb[:, heads, t, :],
-                    in0=q_ps[:].rearrange("p (h d) -> p h d", d=HEAD),
-                    in1=bias_all[:, first : first + PAIR].rearrange("p (h d) -> p h d", d=HEAD),
-                    op=ADD,
+                nc.tensor.matmul(
+                    out=rope_ps[:, t, :], lhsT=straight[:, rows], rhs=ident,
+                    start=True, stop=False, is_transpose=True,
                 )
-            lower = o_sb[:, heads, :, NOPE : NOPE + HALF]
-            upper = o_sb[:, heads, :, NOPE + HALF : HEAD]
-            both = o_sb[:, heads, :, NOPE:HEAD]
-            turned = work.tile([P, 2, T, ROPE], F32)
-            nc.vector.tensor_tensor(
-                out=turned[:, :, :, 0:HALF],
-                in0=upper,
-                in1=sin_sb[:, :, 0:HALF].unsqueeze(1).to_broadcast([P, 2, T, HALF]),
-                op=MULT,
+                nc.tensor.matmul(
+                    out=rope_ps[:, t, :], lhsT=crossed[:, rows], rhs=exchange,
+                    start=False, stop=True, is_transpose=True,
+                )
+            nc.scalar.copy(out=o_sb[:, h, :, NOPE:HEAD], in_=rope_ps[:])
+
+        def nope_pair(m):
+            plain_ps = o_banks.tile([P, T, P], F32, tag="o", name="plain_ps")
+            for t in range(T):
+                nc.tensor.transpose(plain_ps[:, t, :], plain[:, m, t * P : (t + 1) * P], ident)
+            nc.scalar.copy(
+                out=o_sb[:, 2 * m : 2 * m + 2, :, 0:NOPE],
+                in_=plain_ps[:].rearrange("p t (e j) -> p e t j", e=2),
             )
-            nc.vector.tensor_tensor(
-                out=turned[:, :, :, HALF:ROPE],
-                in0=lower,
-                in1=sin_sb[:, :, HALF:ROPE].unsqueeze(1).to_broadcast([P, 2, T, HALF]),
-                op=MULT,
-            )
-            nc.vector.tensor_tensor(
-                out=both,
-                in0=both,
-                in1=cos_sb[:].unsqueeze(1).to_broadcast([P, 2, T, ROPE]),
-                op=MULT,
-            )
-            nc.vector.tensor_tensor(out=both, in0=both, in1=turned[:], op=ADD)
+
+        def store(h):
             nc.sync.dma_start(
-                out=out_v[:, heads, :], in_=o_sb[:, heads, :, :].rearrange("p h t d -> p h (t d)")
+                out=out_v[:, h, :], in_=o_sb[:, h, :, :].rearrange("p t d -> p (t d)")
             )
+
+        for m in range(PAIRS):
+            rope_head(2 * m)
+            nope_pair(m)
+            store(2 * m)
+            rope_head(2 * m + 1)
+            store(2 * m + 1)

@@ -36,8 +36,8 @@ def tile_gptossmlaattention_pb_s_kernel(
     with ExitStack() as ctx:
         keep = ctx.enter_context(tc.tile_pool(name="keep", bufs=1))
         per_head = ctx.enter_context(tc.tile_pool(name="per_head", bufs=HEADS))
-        q_banks = ctx.enter_context(tc.psum_pool(name="q_banks", bufs=4))
-        o_banks = ctx.enter_context(tc.psum_pool(name="o_banks", bufs=4))
+        q_banks = ctx.enter_context(tc.psum_pool(name="q_banks", bufs=3))
+        o_banks = ctx.enter_context(tc.psum_pool(name="o_banks", bufs=5))
         ctx.enter_context(tc.manual_schedule())
 
         bias_rows = keep.tile([P, P], BF16)
@@ -125,41 +125,28 @@ def tile_gptossmlaattention_pb_s_kernel(
         cos_t = tables_t[:, 0, :]
         sin_t = tables_t[:, 1, :]
 
-        def passes(bank, words, scales, first, step):
-            for i in range(2):
-                lo = first + i * step
-                nc.tensor.matmul_mx(
-                    out=bank[:, i, :],
-                    lhsT=words[:, 2 * lo : 2 * (lo + P)].bitcast(FP4X4),
-                    lhsT_scale=scales[:, lo : lo + P],
-                    rhs=x_codes[:].bitcast(FP8X4),
-                    rhs_scale=x_scales[:],
-                    start=True,
-                    stop=True,
-                )
-
-        def rope_passes(m):
-            bank = q_banks.tile([P, 2, SEQ], F32, tag="q", name="rope_q")
-            passes(bank, w_words, w_scales, 2 * m * HEAD + NOPE, HEAD)
-            return bank
-
-        def nope_passes(b):
-            bank = o_banks.tile([P, 2, SEQ], F32, tag="o", name="nope_q")
-            passes(bank, nope_words, nope_scales, 2 * b * P, P)
-            return bank
-
-        rope_q = [rope_passes(0)]
-        nope_q = [nope_passes(b) for b in range(PAIRS // 2)]
-        rope_q.extend([rope_passes(m) for m in range(1, PAIRS)])
-
-        plain = keep.tile([P, PAIRS, SEQ], F32)
-        for m in range(PAIRS):
-            nc.scalar.activation(
-                out=plain[:, m, :],
-                in_=nope_q[m // 2][:, m % 2, :],
-                func=IDENTITY,
-                bias=bias_t[:, HEADS + m : HEADS + m + 1],
+        def one_pass(q_out, words, scales, lo):
+            nc.tensor.matmul_mx(
+                out=q_out,
+                lhsT=words[:, 2 * lo : 2 * (lo + P)].bitcast(FP4X4),
+                lhsT_scale=scales[:, lo : lo + P],
+                rhs=x_codes[:].bitcast(FP8X4),
+                rhs_scale=x_scales[:],
+                start=True,
+                stop=True,
             )
+
+        rope_q = []
+        nope_q = []
+
+        def passes_of_pair(m):
+            bank = q_banks.tile([P, 2, SEQ], F32, tag="q", name="rope_q")
+            for i in range(2):
+                one_pass(bank[:, i, :], w_words, w_scales, (2 * m + i) * HEAD + NOPE)
+            rope_q.append(bank)
+            half_bank = o_banks.tile([P, SEQ], F32, tag="o", name="nope_q")
+            one_pass(half_bank[:], nope_words, nope_scales, m * P)
+            nope_q.append(half_bank)
 
         o_sb = keep.tile([P, HEADS, T, HEAD], F32)
         out_v = out.rearrange("b h (p t) d -> p (b h) (t d)", t=T)
@@ -187,10 +174,18 @@ def tile_gptossmlaattention_pb_s_kernel(
                 )
             nc.scalar.copy(out=o_sb[:, h, :, NOPE:HEAD], in_=rope_ps[:])
 
-        def nope_pair(m):
+        def nope_bias(m):
+            plain = per_head.tile([P, SEQ], F32, name="plain")
+            nc.scalar.activation(
+                out=plain[:], in_=nope_q[m][:], func=IDENTITY,
+                bias=bias_t[:, HEADS + m : HEADS + m + 1],
+            )
+            return plain
+
+        def nope_back(m, plain):
             plain_ps = o_banks.tile([P, T, P], F32, tag="o", name="plain_ps")
             for t in range(T):
-                nc.tensor.transpose(plain_ps[:, t, :], plain[:, m, t * P : (t + 1) * P], ident)
+                nc.tensor.transpose(plain_ps[:, t, :], plain[:, t * P : (t + 1) * P], ident)
             nc.scalar.copy(
                 out=o_sb[:, 2 * m : 2 * m + 2, :, 0:NOPE],
                 in_=plain_ps[:].rearrange("p t (e j) -> p e t j", e=2),
@@ -201,9 +196,13 @@ def tile_gptossmlaattention_pb_s_kernel(
                 out=out_v[:, h, :], in_=o_sb[:, h, :, :].rearrange("p t d -> p (t d)")
             )
 
+        passes_of_pair(0)
         for m in range(PAIRS):
+            if m + 1 < PAIRS:
+                passes_of_pair(m + 1)
+            plain = nope_bias(m)
             rope_head(2 * m)
-            nope_pair(m)
+            nope_back(m, plain)
             store(2 * m)
             rope_head(2 * m + 1)
             store(2 * m + 1)

@@ -36,8 +36,8 @@ def tile_gptossmlaattention_pb_s_kernel(
     with ExitStack() as ctx:
         keep = ctx.enter_context(tc.tile_pool(name="keep", bufs=1))
         per_head = ctx.enter_context(tc.tile_pool(name="per_head", bufs=HEADS))
-        q_banks = ctx.enter_context(tc.psum_pool(name="q_banks", bufs=3))
-        o_banks = ctx.enter_context(tc.psum_pool(name="o_banks", bufs=5))
+        q_banks = ctx.enter_context(tc.psum_pool(name="q_banks", bufs=4))
+        o_banks = ctx.enter_context(tc.psum_pool(name="o_banks", bufs=4))
         ctx.enter_context(tc.manual_schedule())
 
         bias_rows = keep.tile([P, P], BF16)
@@ -125,84 +125,87 @@ def tile_gptossmlaattention_pb_s_kernel(
         cos_t = tables_t[:, 0, :]
         sin_t = tables_t[:, 1, :]
 
-        def one_pass(q_out, words, scales, lo):
+        spread_ps = q_banks.tile([P, PAIRS, P], F32, tag="q")
+        for m in range(PAIRS):
+            nc.tensor.transpose(
+                spread_ps[:, m, :], bias_t[:, HEADS + m : HEADS + m + 1].to_broadcast([P, P]), ident
+            )
+        nope_bias = keep.tile([P, HEADS, NOPE], F32)
+        nc.scalar.copy(
+            out=nope_bias[:].rearrange("p h j -> p (h j)"),
+            in_=spread_ps[:].rearrange("p m i -> p (m i)"),
+        )
+
+        def rope_passes(m):
+            bank = q_banks.tile([P, 2, SEQ], F32, tag="q", name="rope_q")
+            for i in range(2):
+                lo = (2 * m + i) * HEAD + NOPE
+                nc.tensor.matmul_mx(
+                    out=bank[:, i, :],
+                    lhsT=w_words[:, 2 * lo : 2 * (lo + P)].bitcast(FP4X4),
+                    lhsT_scale=w_scales[:, lo : lo + P],
+                    rhs=x_codes[:].bitcast(FP8X4),
+                    rhs_scale=x_scales[:],
+                    start=True,
+                    stop=True,
+                )
+            return bank
+
+        def nope_pass(t):
+            bank = o_banks.tile([P, HEADS, NOPE], F32, tag="o", name="nope_q")
             nc.tensor.matmul_mx(
-                out=q_out,
-                lhsT=words[:, 2 * lo : 2 * (lo + P)].bitcast(FP4X4),
-                lhsT_scale=scales[:, lo : lo + P],
-                rhs=x_codes[:].bitcast(FP8X4),
-                rhs_scale=x_scales[:],
+                out=bank[:].rearrange("p h j -> p (h j)"),
+                lhsT=x_codes[:, t * P : (t + 1) * P].bitcast(FP8X4),
+                lhsT_scale=x_scales[:, t * P : (t + 1) * P],
+                rhs=nope_words[:].bitcast(FP4X4),
+                rhs_scale=nope_scales[:],
                 start=True,
                 stop=True,
             )
+            return bank
 
-        rope_q = []
-        nope_q = []
-
-        def passes_of_pair(m):
-            bank = q_banks.tile([P, 2, SEQ], F32, tag="q", name="rope_q")
-            for i in range(2):
-                one_pass(bank[:, i, :], w_words, w_scales, (2 * m + i) * HEAD + NOPE)
-            rope_q.append(bank)
-            half_bank = o_banks.tile([P, SEQ], F32, tag="o", name="nope_q")
-            one_pass(half_bank[:], nope_words, nope_scales, m * P)
-            nope_q.append(half_bank)
+        rope_q = [rope_passes(0)]
+        nope_q = [nope_pass(t) for t in range(T)]
+        rope_q.extend([rope_passes(m) for m in range(1, PAIRS)])
 
         o_sb = keep.tile([P, HEADS, T, HEAD], F32)
         out_v = out.rearrange("b h (p t) d -> p (b h) (t d)", t=T)
 
-        def rope_head(h):
-            q_t = rope_q[h // 2][:, h % 2, :]
-            straight = per_head.tile([P, SEQ], F32, name="straight")
+        def rope_products(h):
+            products = per_head.tile([P, 2, SEQ], F32, name="products")
             nc.vector.scalar_tensor_tensor(
-                out=straight[:], in0=q_t, scalar=bias_t[:, h : h + 1], in1=cos_t, op0=ADD, op1=MULT
+                out=products[:],
+                in0=rope_q[h // 2][:, h % 2, :].unsqueeze(1).to_broadcast([P, 2, SEQ]),
+                scalar=bias_t[:, h : h + 1],
+                in1=tables_t[:],
+                op0=ADD,
+                op1=MULT,
             )
-            crossed = per_head.tile([P, SEQ], F32, name="crossed")
-            nc.vector.scalar_tensor_tensor(
-                out=crossed[:], in0=q_t, scalar=bias_t[:, h : h + 1], in1=sin_t, op0=ADD, op1=MULT
-            )
+            return products
+
+        def rope_back(h, products):
             rope_ps = o_banks.tile([P, T, P], F32, tag="o", name="rope_ps")
             for t in range(T):
                 rows = slice(t * P, (t + 1) * P)
                 nc.tensor.matmul(
-                    out=rope_ps[:, t, :], lhsT=straight[:, rows], rhs=ident,
+                    out=rope_ps[:, t, :], lhsT=products[:, 0, rows], rhs=ident,
                     start=True, stop=False, is_transpose=True,
                 )
                 nc.tensor.matmul(
-                    out=rope_ps[:, t, :], lhsT=crossed[:, rows], rhs=exchange,
+                    out=rope_ps[:, t, :], lhsT=products[:, 1, rows], rhs=exchange,
                     start=False, stop=True, is_transpose=True,
                 )
             nc.scalar.copy(out=o_sb[:, h, :, NOPE:HEAD], in_=rope_ps[:])
-
-        def nope_bias(m):
-            plain = per_head.tile([P, SEQ], F32, name="plain")
-            nc.scalar.activation(
-                out=plain[:], in_=nope_q[m][:], func=IDENTITY,
-                bias=bias_t[:, HEADS + m : HEADS + m + 1],
-            )
-            return plain
-
-        def nope_back(m, plain):
-            plain_ps = o_banks.tile([P, T, P], F32, tag="o", name="plain_ps")
-            for t in range(T):
-                nc.tensor.transpose(plain_ps[:, t, :], plain[:, t * P : (t + 1) * P], ident)
-            nc.scalar.copy(
-                out=o_sb[:, 2 * m : 2 * m + 2, :, 0:NOPE],
-                in_=plain_ps[:].rearrange("p t (e j) -> p e t j", e=2),
-            )
-
-        def store(h):
             nc.sync.dma_start(
                 out=out_v[:, h, :], in_=o_sb[:, h, :, :].rearrange("p t d -> p (t d)")
             )
 
-        passes_of_pair(0)
-        for m in range(PAIRS):
-            if m + 1 < PAIRS:
-                passes_of_pair(m + 1)
-            plain = nope_bias(m)
-            rope_head(2 * m)
-            nope_back(m, plain)
-            store(2 * m)
-            rope_head(2 * m + 1)
-            store(2 * m + 1)
+        first_pair = [rope_products(h) for h in range(2)]
+        for t in range(T):
+            nc.vector.tensor_tensor(
+                out=o_sb[:, :, t, 0:NOPE], in0=nope_q[t][:], in1=nope_bias[:], op=ADD
+            )
+        for h in range(2):
+            rope_back(h, first_pair[h])
+        for h in range(2, HEADS):
+            rope_back(h, rope_products(h))

@@ -46,8 +46,11 @@ def tile_gptossmlaattention_pb_s_kernel(
         nc.vector.memset(w_scales[:].bitcast(I32), 0)
         warm = keep.tile([P, 1], F32)
         nc.vector.memset(warm[:], 0.0)
-        nc.scalar.activation(out=warm[:], in_=warm[:], func=IDENTITY)
 
+        cos_sb = keep.tile([P, T, ROPE], BF16)
+        nc.scalar.dma_start(out=cos_sb[:], in_=cos.rearrange("b (p t) j -> p (b t) j", t=T))
+        sin_sb = keep.tile([P, T, ROPE], BF16)
+        nc.scalar.dma_start(out=sin_sb[:], in_=sin.rearrange("b (p t) j -> p (b t) j", t=T))
         nc.scalar.dma_start(
             out=bias_rows[0:HEADS, :], in_=bq.rearrange("(h d) -> h d", d=HEAD)[:, NOPE:HEAD]
         )
@@ -55,6 +58,7 @@ def tile_gptossmlaattention_pb_s_kernel(
             out=bias_rows[HEADS : HEADS + PAIRS, :].rearrange("m (e j) -> m e j", e=2),
             in_=bq.rearrange("(m e d) -> m e d", e=2, d=HEAD)[:, :, 0:NOPE],
         )
+        nc.scalar.activation(out=warm[:], in_=warm[:], func=IDENTITY)
         x_sb = keep.tile([P, T, HID], BF16)
         nc.sync.dma_start(
             out=x_sb[:], in_=hidden_states.rearrange("b (p t) k -> p (b t) k", t=T)
@@ -66,10 +70,6 @@ def tile_gptossmlaattention_pb_s_kernel(
             )
         w_words = keep.tile([P, 2 * N_OUT], U8, align_bytes=64)
         nc.sync.dma_start(out=w_words[:].bitcast(I32), in_=Wq_words[0].bitcast(I32))
-        cos_sb = keep.tile([P, T, ROPE], BF16)
-        nc.scalar.dma_start(out=cos_sb[:], in_=cos.rearrange("b (p t) j -> p (b t) j", t=T))
-        sin_sb = keep.tile([P, T, ROPE], BF16)
-        nc.scalar.dma_start(out=sin_sb[:], in_=sin.rearrange("b (p t) j -> p (b t) j", t=T))
 
         eye = keep.tile([P, HALF + P], F32)
         make_identity(nc, eye[:, HALF : HALF + P])

@@ -25,6 +25,8 @@ HEAD = NOPE + ROPE
 N_OUT = HEADS * HEAD
 T = SEQ // P
 PAIRS = HEADS // 2
+GPSIMD_HEADS = (0, 1, 2)
+BACK_ORDER = (0, 3, 4, 1, 5, 6, 2, 7)
 
 FLOPS = 2 * SEQ * HID * N_OUT
 
@@ -40,12 +42,24 @@ def tile_gptossmlaattention_pb_s_kernel(
         o_banks = ctx.enter_context(tc.psum_pool(name="o_banks", bufs=4))
         ctx.enter_context(tc.manual_schedule())
 
-        bias_rows = keep.tile([P, P], BF16)
-        nc.vector.memset(bias_rows[:], 0.0)
+        zeros = keep.tile([P, 2 * P], F32)
+        nc.gpsimd.memset(zeros[:], 0.0)
+        idle_ps = q_banks.tile([P, 2 * P], F32, tag="q")
+        for rep in range(2):
+            nc.tensor.matmul(
+                out=idle_ps[:], lhsT=zeros[:, 0:P], rhs=zeros[:], start=True, stop=True
+            )
+
         w_scales = keep.tile([P, N_OUT], U8, align_bytes=64)
         nc.vector.memset(w_scales[:].bitcast(I32), 0)
+        bias_rows = keep.tile([P, P], BF16)
+        nc.vector.memset(bias_rows[:], 0.0)
+        nope_bias_row = keep.tile([P, HEADS * NOPE], BF16)
+        nc.vector.memset(nope_bias_row[:], 0.0)
         warm = keep.tile([P, 1], F32)
         nc.vector.memset(warm[:], 0.0)
+        ones = keep.tile([P, P], BF16)
+        nc.vector.memset(ones[:], 1.0)
 
         cos_sb = keep.tile([P, T, ROPE], BF16)
         nc.scalar.dma_start(out=cos_sb[:], in_=cos.rearrange("b (p t) j -> p (b t) j", t=T))
@@ -54,22 +68,22 @@ def tile_gptossmlaattention_pb_s_kernel(
         nc.scalar.dma_start(
             out=bias_rows[0:HEADS, :], in_=bq.rearrange("(h d) -> h d", d=HEAD)[:, NOPE:HEAD]
         )
-        nc.scalar.dma_start(
-            out=bias_rows[HEADS : HEADS + PAIRS, :].rearrange("m (e j) -> m e j", e=2),
-            in_=bq.rearrange("(m e d) -> m e d", e=2, d=HEAD)[:, :, 0:NOPE],
-        )
         nc.scalar.activation(out=warm[:], in_=warm[:], func=IDENTITY)
         x_sb = keep.tile([P, T, HID], BF16)
         nc.sync.dma_start(
             out=x_sb[:], in_=hidden_states.rearrange("b (p t) k -> p (b t) k", t=T)
         )
+        w_words = keep.tile([P, 2 * N_OUT], U8, align_bytes=64)
+        nc.sync.dma_start(out=w_words[:].bitcast(I32), in_=Wq_words[0].bitcast(I32))
         for quad in range(4):
             nc.sync.dma_start(
                 out=w_scales[32 * quad : 32 * quad + 4, :].bitcast(I32),
                 in_=Wq_scales[0, 4 * quad : 4 * quad + 4, :].bitcast(I32),
             )
-        w_words = keep.tile([P, 2 * N_OUT], U8, align_bytes=64)
-        nc.sync.dma_start(out=w_words[:].bitcast(I32), in_=Wq_words[0].bitcast(I32))
+        nc.sync.dma_start(
+            out=nope_bias_row[0:1, :].rearrange("o (h j) -> o h j", h=HEADS),
+            in_=bq.rearrange("(o h d) -> o h d", o=1, d=HEAD)[:, :, 0:NOPE],
+        )
 
         eye = keep.tile([P, HALF + P], F32)
         make_identity(nc, eye[:, HALF : HALF + P])
@@ -78,6 +92,12 @@ def tile_gptossmlaattention_pb_s_kernel(
         ident_bf = keep.tile([P, P], BF16)
         make_identity(nc, ident_bf[:])
         nc.gpsimd.tensor_copy(out=eye[:, 0:HALF], in_=eye[:, P : P + HALF])
+
+        sin_x = keep.tile([P, T, ROPE], BF16)
+        nc.vector.tensor_copy(out=sin_x[:, :, 0:HALF], in_=sin_sb[:, :, HALF:ROPE])
+        nc.vector.tensor_scalar(
+            out=sin_x[:, :, HALF:ROPE], in0=sin_sb[:, :, 0:HALF], scalar1=-1.0, scalar2=None, op0=MULT
+        )
 
         x_words = x_sb[:].bitcast(F32)
         xt_ps = o_banks.tile([P, 2, SEQ], F32, tag="o")
@@ -109,11 +129,8 @@ def tile_gptossmlaattention_pb_s_kernel(
 
         bias_ps = q_banks.tile([P, P], BF16, tag="q")
         nc.tensor.transpose(bias_ps[:], bias_rows[:], ident_bf[:])
-        bias_t = keep.tile([P, HEADS + PAIRS], F32)
-        nc.scalar.copy(out=bias_t[:], in_=bias_ps[:, 0 : HEADS + PAIRS])
-        sin_x = keep.tile([P, T, ROPE], BF16)
-        nc.scalar.copy(out=sin_x[:, :, 0:HALF], in_=sin_sb[:, :, HALF:ROPE])
-        nc.scalar.mul(out=sin_x[:, :, HALF:ROPE], in_=sin_sb[:, :, 0:HALF], mul=-1.0)
+        bias_t = keep.tile([P, HEADS], F32)
+        nc.scalar.copy(out=bias_t[:], in_=bias_ps[:, 0:HEADS])
         tables_ps = o_banks.tile([P, 2, SEQ], BF16, tag="o")
         for t in range(T):
             nc.tensor.transpose(tables_ps[:, 0, t * P : (t + 1) * P], cos_sb[:, t, :], ident_bf[:])
@@ -122,19 +139,11 @@ def tile_gptossmlaattention_pb_s_kernel(
         tables_t = keep.tile([P, 2, SEQ], BF16)
         nc.scalar.copy(out=tables_t[:, 0, :], in_=tables_ps[:, 0, :])
         nc.scalar.copy(out=tables_t[:, 1, :], in_=tables_ps[:, 1, :])
-        cos_t = tables_t[:, 0, :]
-        sin_t = tables_t[:, 1, :]
 
-        spread_ps = q_banks.tile([P, PAIRS, P], F32, tag="q")
-        for m in range(PAIRS):
-            nc.tensor.transpose(
-                spread_ps[:, m, :], bias_t[:, HEADS + m : HEADS + m + 1].to_broadcast([P, P]), ident
-            )
+        spread_ps = q_banks.tile([P, HEADS * NOPE], F32, tag="q")
+        nc.tensor.matmul(out=spread_ps[:], lhsT=ones[:], rhs=nope_bias_row[:], start=True, stop=True)
         nope_bias = keep.tile([P, HEADS, NOPE], F32)
-        nc.scalar.copy(
-            out=nope_bias[:].rearrange("p h j -> p (h j)"),
-            in_=spread_ps[:].rearrange("p m i -> p (m i)"),
-        )
+        nc.vector.tensor_copy(out=nope_bias[:].rearrange("p h j -> p (h j)"), in_=spread_ps[:])
 
         def rope_passes(m):
             bank = q_banks.tile([P, 2, SEQ], F32, tag="q", name="rope_q")
@@ -173,14 +182,27 @@ def tile_gptossmlaattention_pb_s_kernel(
 
         def rope_products(h):
             products = per_head.tile([P, 2, SEQ], F32, name="products")
-            nc.vector.scalar_tensor_tensor(
-                out=products[:],
-                in0=rope_q[h // 2][:, h % 2, :].unsqueeze(1).to_broadcast([P, 2, SEQ]),
-                scalar=bias_t[:, h : h + 1],
-                in1=tables_t[:],
-                op0=ADD,
-                op1=MULT,
-            )
+            q_h = rope_q[h // 2][:, h % 2, :]
+            if h in GPSIMD_HEADS:
+                y_sb = per_head.tile([P, SEQ], F32, name="y_sb")
+                nc.scalar.activation(
+                    out=y_sb[:], in_=q_h, func=IDENTITY, bias=bias_t[:, h : h + 1], scale=1.0
+                )
+                nc.gpsimd.tensor_tensor(
+                    out=products[:],
+                    in0=y_sb[:].unsqueeze(1).to_broadcast([P, 2, SEQ]),
+                    in1=tables_t[:],
+                    op=MULT,
+                )
+            else:
+                nc.vector.scalar_tensor_tensor(
+                    out=products[:],
+                    in0=q_h.unsqueeze(1).to_broadcast([P, 2, SEQ]),
+                    scalar=bias_t[:, h : h + 1],
+                    in1=tables_t[:],
+                    op0=ADD,
+                    op1=MULT,
+                )
             return products
 
         def rope_back(h, products):
@@ -200,12 +222,14 @@ def tile_gptossmlaattention_pb_s_kernel(
                 out=out_v[:, h, :], in_=o_sb[:, h, :, :].rearrange("p t d -> p (t d)")
             )
 
-        first_pair = [rope_products(h) for h in range(2)]
+        products_of = {}
+        for h in GPSIMD_HEADS:
+            products_of[h] = rope_products(h)
         for t in range(T):
             nc.vector.tensor_tensor(
                 out=o_sb[:, :, t, 0:NOPE], in0=nope_q[t][:], in1=nope_bias[:], op=ADD
             )
-        for h in range(2):
-            rope_back(h, first_pair[h])
-        for h in range(2, HEADS):
-            rope_back(h, rope_products(h))
+        for h in BACK_ORDER:
+            if h not in GPSIMD_HEADS:
+                products_of[h] = rope_products(h)
+            rope_back(h, products_of[h])

@@ -26,7 +26,8 @@ N_OUT = HEADS * HEAD
 T = SEQ // P
 PAIRS = HEADS // 2
 GPSIMD_HEADS = (0, 1, 2)
-BACK_ORDER = (0, 3, 4, 1, 5, 6, 2, 7)
+IDLE_N = 224
+BACK_ORDER = (4, 0, 5, 3, 1, 6, 7, 2)
 
 FLOPS = 2 * SEQ * HID * N_OUT
 
@@ -42,9 +43,9 @@ def tile_gptossmlaattention_pb_s_kernel(
         o_banks = ctx.enter_context(tc.psum_pool(name="o_banks", bufs=4))
         ctx.enter_context(tc.manual_schedule())
 
-        zeros = keep.tile([P, 2 * P], F32)
+        zeros = keep.tile([P, IDLE_N], F32)
         nc.gpsimd.memset(zeros[:], 0.0)
-        idle_ps = q_banks.tile([P, 2 * P], F32, tag="q")
+        idle_ps = q_banks.tile([P, IDLE_N], F32, tag="q")
         for rep in range(2):
             nc.tensor.matmul(
                 out=idle_ps[:], lhsT=zeros[:, 0:P], rhs=zeros[:], start=True, stop=True
@@ -100,22 +101,23 @@ def tile_gptossmlaattention_pb_s_kernel(
         )
 
         x_words = x_sb[:].bitcast(F32)
-        xt_ps = o_banks.tile([P, 2, SEQ], F32, tag="o")
-        for t in range(T):
-            for u in range(2):
-                nc.tensor.transpose(
-                    xt_ps[:, u, t * P : (t + 1) * P], x_words[:, t, u : HID // 2 : 2], ident
-                )
-        x_grouped = keep.tile([P, 4 * SEQ], BF16, align_bytes=64)
-        nc.vector.tensor_copy(
-            out=x_grouped[:].bitcast(F32).rearrange("p (c u) -> p c u", u=2),
-            in_=xt_ps[:].rearrange("p u c -> p c u"),
-        )
+        x_grouped = keep.tile([P, T, 4 * P], BF16, align_bytes=64)
         x_codes = keep.tile([P, SEQ], U32, align_bytes=64)
         x_scales = keep.tile([P, SEQ], U8, align_bytes=64)
-        nc.vector.quantize_mx(
-            out=x_codes[:].bitcast(FP8X4), scales=x_scales[:], in_=x_grouped[:]
-        )
+        for t in range(T):
+            xt_ps = o_banks.tile([P, 2, P], F32, tag="o", name="xt_ps")
+            for u in range(2):
+                nc.tensor.transpose(xt_ps[:, u, :], x_words[:, t, u : HID // 2 : 2], ident)
+            copy_out = nc.vector.tensor_copy if t == 0 else nc.scalar.copy
+            copy_out(
+                out=x_grouped[:, t, :].bitcast(F32).rearrange("p (c u) -> p c u", u=2),
+                in_=xt_ps[:].rearrange("p u c -> p c u"),
+            )
+        for t in range(T):
+            cols = slice(t * P, (t + 1) * P)
+            nc.vector.quantize_mx(
+                out=x_codes[:, cols].bitcast(FP8X4), scales=x_scales[:, cols], in_=x_grouped[:, t, :]
+            )
         nope_words = keep.tile([P, 2 * HEADS * NOPE], U8, align_bytes=64)
         nc.vector.tensor_copy(
             out=nope_words[:].bitcast(I32).rearrange("p (h w) -> p h w", h=HEADS),
@@ -145,20 +147,19 @@ def tile_gptossmlaattention_pb_s_kernel(
         nope_bias = keep.tile([P, HEADS, NOPE], F32)
         nc.vector.tensor_copy(out=nope_bias[:].rearrange("p h j -> p (h j)"), in_=spread_ps[:])
 
-        def rope_passes(m):
-            bank = q_banks.tile([P, 2, SEQ], F32, tag="q", name="rope_q")
-            for i in range(2):
-                lo = (2 * m + i) * HEAD + NOPE
-                nc.tensor.matmul_mx(
-                    out=bank[:, i, :],
-                    lhsT=w_words[:, 2 * lo : 2 * (lo + P)].bitcast(FP4X4),
-                    lhsT_scale=w_scales[:, lo : lo + P],
-                    rhs=x_codes[:].bitcast(FP8X4),
-                    rhs_scale=x_scales[:],
-                    start=True,
-                    stop=True,
-                )
-            return bank
+        rope_q = [q_banks.tile([P, 2, SEQ], F32, tag="q", name="rope_q") for m in range(PAIRS)]
+
+        def rope_pass(h):
+            lo = h * HEAD + NOPE
+            nc.tensor.matmul_mx(
+                out=rope_q[h // 2][:, h % 2, :],
+                lhsT=w_words[:, 2 * lo : 2 * (lo + P)].bitcast(FP4X4),
+                lhsT_scale=w_scales[:, lo : lo + P],
+                rhs=x_codes[:].bitcast(FP8X4),
+                rhs_scale=x_scales[:],
+                start=True,
+                stop=True,
+            )
 
         def nope_pass(t):
             bank = o_banks.tile([P, HEADS, NOPE], F32, tag="o", name="nope_q")
@@ -173,9 +174,11 @@ def tile_gptossmlaattention_pb_s_kernel(
             )
             return bank
 
-        rope_q = [rope_passes(0)]
+        for h in (0, 1, 4, 5):
+            rope_pass(h)
         nope_q = [nope_pass(t) for t in range(T)]
-        rope_q.extend([rope_passes(m) for m in range(1, PAIRS)])
+        for h in (2, 3, 6, 7):
+            rope_pass(h)
 
         o_sb = keep.tile([P, HEADS, T, HEAD], F32)
         out_v = out.rearrange("b h (p t) d -> p (b h) (t d)", t=T)
@@ -225,11 +228,12 @@ def tile_gptossmlaattention_pb_s_kernel(
         products_of = {}
         for h in GPSIMD_HEADS:
             products_of[h] = rope_products(h)
+        products_of[4] = rope_products(4)
         for t in range(T):
             nc.vector.tensor_tensor(
                 out=o_sb[:, :, t, 0:NOPE], in0=nope_q[t][:], in1=nope_bias[:], op=ADD
             )
         for h in BACK_ORDER:
-            if h not in GPSIMD_HEADS:
+            if h not in products_of:
                 products_of[h] = rope_products(h)
             rope_back(h, products_of[h])

@@ -51,28 +51,32 @@ def tile_gptossmlaattention_pb_s_kernel(
                 out=idle_ps[:], lhsT=zeros[:, 0:P], rhs=zeros[:], start=True, stop=True
             )
 
+        biases = keep.tile([P, HEADS * NOPE + P], BF16)
+        nc.vector.memset(biases[:].bitcast(I32), 0)
+        nope_bias_row = biases[:, 0 : HEADS * NOPE]
+        bias_rows = biases[:, HEADS * NOPE : HEADS * NOPE + P]
         w_scales = keep.tile([P, N_OUT], U8, align_bytes=64)
         nc.vector.memset(w_scales[:].bitcast(I32), 0)
-        bias_rows = keep.tile([P, P], BF16)
-        nc.vector.memset(bias_rows[:], 0.0)
-        nope_bias_row = keep.tile([P, HEADS * NOPE], BF16)
-        nc.vector.memset(nope_bias_row[:], 0.0)
-        warm = keep.tile([P, 1], F32)
-        nc.vector.memset(warm[:], 0.0)
         ones = keep.tile([P, P], BF16)
         nc.vector.memset(ones[:], 1.0)
+        warm = keep.tile([P, 1], F32)
+        nc.vector.memset(warm[:], 0.0)
 
         cos_sb = keep.tile([P, T, ROPE], BF16)
         nc.scalar.dma_start(out=cos_sb[:], in_=cos.rearrange("b (p t) j -> p (b t) j", t=T))
         sin_sb = keep.tile([P, T, ROPE], BF16)
         nc.scalar.dma_start(out=sin_sb[:], in_=sin.rearrange("b (p t) j -> p (b t) j", t=T))
-        nc.scalar.dma_start(
-            out=bias_rows[0:HEADS, :], in_=bq.rearrange("(h d) -> h d", d=HEAD)[:, NOPE:HEAD]
-        )
         nc.scalar.activation(out=warm[:], in_=warm[:], func=IDENTITY)
         x_sb = keep.tile([P, T, HID], BF16)
         nc.sync.dma_start(
             out=x_sb[:], in_=hidden_states.rearrange("b (p t) k -> p (b t) k", t=T)
+        )
+        nc.sync.dma_start(
+            out=bias_rows[0:HEADS, :], in_=bq.rearrange("(h d) -> h d", d=HEAD)[:, NOPE:HEAD]
+        )
+        nc.sync.dma_start(
+            out=nope_bias_row[0:1, :].rearrange("o (h j) -> o h j", h=HEADS),
+            in_=bq.rearrange("(o h d) -> o h d", o=1, d=HEAD)[:, :, 0:NOPE],
         )
         w_words = keep.tile([P, 2 * N_OUT], U8, align_bytes=64)
         nc.sync.dma_start(out=w_words[:].bitcast(I32), in_=Wq_words[0].bitcast(I32))
@@ -81,10 +85,6 @@ def tile_gptossmlaattention_pb_s_kernel(
                 out=w_scales[32 * quad : 32 * quad + 4, :].bitcast(I32),
                 in_=Wq_scales[0, 4 * quad : 4 * quad + 4, :].bitcast(I32),
             )
-        nc.sync.dma_start(
-            out=nope_bias_row[0:1, :].rearrange("o (h j) -> o h j", h=HEADS),
-            in_=bq.rearrange("(o h d) -> o h d", o=1, d=HEAD)[:, :, 0:NOPE],
-        )
 
         eye = keep.tile([P, HALF + P], F32)
         make_identity(nc, eye[:, HALF : HALF + P])
@@ -93,12 +93,6 @@ def tile_gptossmlaattention_pb_s_kernel(
         ident_bf = keep.tile([P, P], BF16)
         make_identity(nc, ident_bf[:])
         nc.gpsimd.tensor_copy(out=eye[:, 0:HALF], in_=eye[:, P : P + HALF])
-
-        sin_x = keep.tile([P, T, ROPE], BF16)
-        nc.vector.tensor_copy(out=sin_x[:, :, 0:HALF], in_=sin_sb[:, :, HALF:ROPE])
-        nc.vector.tensor_scalar(
-            out=sin_x[:, :, HALF:ROPE], in0=sin_sb[:, :, 0:HALF], scalar1=-1.0, scalar2=None, op0=MULT
-        )
 
         x_words = x_sb[:].bitcast(F32)
         x_grouped = keep.tile([P, T, 4 * P], BF16, align_bytes=64)
@@ -113,6 +107,21 @@ def tile_gptossmlaattention_pb_s_kernel(
                 out=x_grouped[:, t, :].bitcast(F32).rearrange("p (c u) -> p c u", u=2),
                 in_=xt_ps[:].rearrange("p u c -> p c u"),
             )
+
+        bias_ps = q_banks.tile([P, HEADS], F32, tag="q")
+        nc.tensor.matmul(
+            out=bias_ps[:], lhsT=bias_rows, rhs=ident_bf[:, 0:HEADS], start=True, stop=True
+        )
+        bias_t = keep.tile([P, HEADS], F32)
+        nc.scalar.copy(out=bias_t[:], in_=bias_ps[:])
+        spread_ps = q_banks.tile([P, HEADS * NOPE], F32, tag="q")
+        nc.tensor.matmul(out=spread_ps[:], lhsT=ones[:], rhs=nope_bias_row, start=True, stop=True)
+
+        sin_x = keep.tile([P, T, ROPE], BF16)
+        nc.vector.tensor_copy(out=sin_x[:, :, 0:HALF], in_=sin_sb[:, :, HALF:ROPE])
+        nc.vector.tensor_scalar(
+            out=sin_x[:, :, HALF:ROPE], in0=sin_sb[:, :, 0:HALF], scalar1=-1.0, scalar2=None, op0=MULT
+        )
         for t in range(T):
             cols = slice(t * P, (t + 1) * P)
             nc.vector.quantize_mx(
@@ -129,10 +138,9 @@ def tile_gptossmlaattention_pb_s_kernel(
             in_=w_scales[:].bitcast(I32).rearrange("p (h w) -> p h w", h=HEADS)[:, :, 0 : NOPE // 4],
         )
 
-        bias_ps = q_banks.tile([P, P], BF16, tag="q")
-        nc.tensor.transpose(bias_ps[:], bias_rows[:], ident_bf[:])
-        bias_t = keep.tile([P, HEADS], F32)
-        nc.scalar.copy(out=bias_t[:], in_=bias_ps[:, 0:HEADS])
+        nope_bias = keep.tile([P, HEADS, NOPE], F32)
+        nc.vector.tensor_copy(out=nope_bias[:].rearrange("p h j -> p (h j)"), in_=spread_ps[:])
+
         tables_ps = o_banks.tile([P, 2, SEQ], BF16, tag="o")
         for t in range(T):
             nc.tensor.transpose(tables_ps[:, 0, t * P : (t + 1) * P], cos_sb[:, t, :], ident_bf[:])
@@ -141,11 +149,6 @@ def tile_gptossmlaattention_pb_s_kernel(
         tables_t = keep.tile([P, 2, SEQ], BF16)
         nc.scalar.copy(out=tables_t[:, 0, :], in_=tables_ps[:, 0, :])
         nc.scalar.copy(out=tables_t[:, 1, :], in_=tables_ps[:, 1, :])
-
-        spread_ps = q_banks.tile([P, HEADS * NOPE], F32, tag="q")
-        nc.tensor.matmul(out=spread_ps[:], lhsT=ones[:], rhs=nope_bias_row[:], start=True, stop=True)
-        nope_bias = keep.tile([P, HEADS, NOPE], F32)
-        nc.vector.tensor_copy(out=nope_bias[:].rearrange("p h j -> p (h j)"), in_=spread_ps[:])
 
         rope_q = [q_banks.tile([P, 2, SEQ], F32, tag="q", name="rope_q") for m in range(PAIRS)]
 

@@ -24,10 +24,12 @@ HALF = ROPE // 2
 HEAD = NOPE + ROPE
 N_OUT = HEADS * HEAD
 T = SEQ // P
-PAIRS = HEADS // 2
-GPSIMD_HEADS = (0, 1, 2)
+GPSIMD_SETS = {0: (0, 1), 1: (0, 1), 2: (0,)}
 IDLE_N = 224
-BACK_ORDER = (4, 0, 5, 3, 1, 6, 7, 2)
+BACK_ORDER = (
+    (4, (0, 1)), (0, (0, 1)), (5, (0, 1)), (3, (0, 1)), (1, (0, 1)), (6, (0, 1)), (2, (0, 1)),
+    (7, (0,)), (7, (1,)),
+)
 
 FLOPS = 2 * SEQ * HID * N_OUT
 
@@ -39,8 +41,8 @@ def tile_gptossmlaattention_pb_s_kernel(
     with ExitStack() as ctx:
         keep = ctx.enter_context(tc.tile_pool(name="keep", bufs=1))
         per_head = ctx.enter_context(tc.tile_pool(name="per_head", bufs=HEADS))
-        q_banks = ctx.enter_context(tc.psum_pool(name="q_banks", bufs=4))
-        o_banks = ctx.enter_context(tc.psum_pool(name="o_banks", bufs=4))
+        q_banks = ctx.enter_context(tc.psum_pool(name="q_banks", bufs=5))
+        o_banks = ctx.enter_context(tc.psum_pool(name="o_banks", bufs=3))
         ctx.enter_context(tc.manual_schedule())
 
         zeros = keep.tile([P, IDLE_N], F32)
@@ -150,12 +152,16 @@ def tile_gptossmlaattention_pb_s_kernel(
         nc.scalar.copy(out=tables_t[:, 0, :], in_=tables_ps[:, 0, :])
         nc.scalar.copy(out=tables_t[:, 1, :], in_=tables_ps[:, 1, :])
 
-        rope_q = [q_banks.tile([P, 2, SEQ], F32, tag="q", name="rope_q") for m in range(PAIRS)]
+        rope_q = {}
+        for heads in ((0,), (4,), (1, 2), (3, 5), (6, 7)):
+            bank = q_banks.tile([P, 2, SEQ], F32, tag="q", name="rope_q")
+            for i, h in enumerate(heads):
+                rope_q[h] = bank[:, i, :]
 
         def rope_pass(h):
             lo = h * HEAD + NOPE
             nc.tensor.matmul_mx(
-                out=rope_q[h // 2][:, h % 2, :],
+                out=rope_q[h],
                 lhsT=w_words[:, 2 * lo : 2 * (lo + P)].bitcast(FP4X4),
                 lhsT_scale=w_scales[:, lo : lo + P],
                 rhs=x_codes[:].bitcast(FP8X4),
@@ -177,66 +183,71 @@ def tile_gptossmlaattention_pb_s_kernel(
             )
             return bank
 
-        for h in (0, 1, 4, 5):
+        for h in (0, 4):
             rope_pass(h)
         nope_q = [nope_pass(t) for t in range(T)]
-        for h in (2, 3, 6, 7):
+        for h in (1, 5, 3, 2, 6, 7):
             rope_pass(h)
 
         o_sb = keep.tile([P, HEADS, T, HEAD], F32)
-        out_v = out.rearrange("b h (p t) d -> p (b h) (t d)", t=T)
+        out_v = out.rearrange("b h (p t) d -> p (b h) t d", t=T)
+        products = {
+            h: per_head.tile([P, 2, SEQ], F32, tag="products", name="products") for h in range(HEADS)
+        }
 
-        def rope_products(h):
-            products = per_head.tile([P, 2, SEQ], F32, name="products")
-            q_h = rope_q[h // 2][:, h % 2, :]
-            if h in GPSIMD_HEADS:
-                y_sb = per_head.tile([P, SEQ], F32, name="y_sb")
-                nc.scalar.activation(
-                    out=y_sb[:], in_=q_h, func=IDENTITY, bias=bias_t[:, h : h + 1], scale=1.0
-                )
-                nc.gpsimd.tensor_tensor(
-                    out=products[:],
-                    in0=y_sb[:].unsqueeze(1).to_broadcast([P, 2, SEQ]),
-                    in1=tables_t[:],
-                    op=MULT,
-                )
-            else:
-                nc.vector.scalar_tensor_tensor(
-                    out=products[:],
-                    in0=q_h.unsqueeze(1).to_broadcast([P, 2, SEQ]),
-                    scalar=bias_t[:, h : h + 1],
-                    in1=tables_t[:],
-                    op0=ADD,
-                    op1=MULT,
-                )
-            return products
+        def gpsimd_products(h):
+            width = len(GPSIMD_SETS[h]) * P
+            y_sb = per_head.tile([P, SEQ], F32, name="y_sb")
+            nc.scalar.activation(
+                out=y_sb[:, 0:width],
+                in_=rope_q[h][:, 0:width],
+                func=IDENTITY,
+                bias=bias_t[:, h : h + 1],
+                scale=1.0,
+            )
+            nc.gpsimd.tensor_tensor(
+                out=products[h][:, :, 0:width],
+                in0=y_sb[:, 0:width].unsqueeze(1).to_broadcast([P, 2, width]),
+                in1=tables_t[:, :, 0:width],
+                op=MULT,
+            )
 
-        def rope_back(h, products):
+        def vector_products(h, sets):
+            cols = slice(sets[0] * P, (sets[-1] + 1) * P)
+            width = len(sets) * P
+            nc.vector.scalar_tensor_tensor(
+                out=products[h][:, :, cols],
+                in0=rope_q[h][:, cols].unsqueeze(1).to_broadcast([P, 2, width]),
+                scalar=bias_t[:, h : h + 1],
+                in1=tables_t[:, :, cols],
+                op0=ADD,
+                op1=MULT,
+            )
+
+        def rope_back(h, sets, copy_out):
             rope_ps = o_banks.tile([P, T, P], F32, tag="o", name="rope_ps")
-            for t in range(T):
+            for t in sets:
                 rows = slice(t * P, (t + 1) * P)
                 nc.tensor.matmul(
-                    out=rope_ps[:, t, :], lhsT=products[:, 0, rows], rhs=ident,
+                    out=rope_ps[:, t, :], lhsT=products[h][:, 0, rows], rhs=ident,
                     start=True, stop=False, is_transpose=True,
                 )
                 nc.tensor.matmul(
-                    out=rope_ps[:, t, :], lhsT=products[:, 1, rows], rhs=exchange,
+                    out=rope_ps[:, t, :], lhsT=products[h][:, 1, rows], rhs=exchange,
                     start=False, stop=True, is_transpose=True,
                 )
-            nc.scalar.copy(out=o_sb[:, h, :, NOPE:HEAD], in_=rope_ps[:])
-            nc.sync.dma_start(
-                out=out_v[:, h, :], in_=o_sb[:, h, :, :].rearrange("p t d -> p (t d)")
-            )
+            done = slice(sets[0], sets[-1] + 1)
+            copy_out(out=o_sb[:, h, done, NOPE:HEAD], in_=rope_ps[:, done, :])
+            nc.sync.dma_start(out=out_v[:, h, done, :], in_=o_sb[:, h, done, :])
 
-        products_of = {}
-        for h in GPSIMD_HEADS:
-            products_of[h] = rope_products(h)
-        products_of[4] = rope_products(4)
+        for h in GPSIMD_SETS:
+            gpsimd_products(h)
+        vector_products(4, (0, 1))
         for t in range(T):
             nc.vector.tensor_tensor(
                 out=o_sb[:, :, t, 0:NOPE], in0=nope_q[t][:], in1=nope_bias[:], op=ADD
             )
-        for h in BACK_ORDER:
-            if h not in products_of:
-                products_of[h] = rope_products(h)
-            rope_back(h, products_of[h])
+        for h, sets in ((5, (0, 1)), (3, (0, 1)), (6, (0, 1)), (2, (1,)), (7, (0,)), (7, (1,))):
+            vector_products(h, sets)
+        for h, sets in BACK_ORDER:
+            rope_back(h, sets, nc.vector.tensor_copy if (h, sets) == BACK_ORDER[-1] else nc.scalar.copy)

@@ -64,15 +64,15 @@ def tile_gptossmlaattention_pb_s_kernel(
         warm = keep.tile([P, 1], F32)
         nc.vector.memset(warm[:], 0.0)
 
-        cos_sb = keep.tile([P, T, ROPE], BF16)
-        nc.scalar.dma_start(out=cos_sb[:], in_=cos.rearrange("b (p t) j -> p (b t) j", t=T))
-        sin_sb = keep.tile([P, T, ROPE], BF16)
-        nc.scalar.dma_start(out=sin_sb[:], in_=sin.rearrange("b (p t) j -> p (b t) j", t=T))
         nc.scalar.activation(out=warm[:], in_=warm[:], func=IDENTITY)
         x_sb = keep.tile([P, T, HID], BF16)
         nc.sync.dma_start(
             out=x_sb[:], in_=hidden_states.rearrange("b (p t) k -> p (b t) k", t=T)
         )
+        cos_sb = keep.tile([P, T, ROPE], BF16)
+        nc.sync.dma_start(out=cos_sb[:], in_=cos.rearrange("b (p t) j -> p (b t) j", t=T))
+        sin_sb = keep.tile([P, T, ROPE], BF16)
+        nc.sync.dma_start(out=sin_sb[:], in_=sin.rearrange("b (p t) j -> p (b t) j", t=T))
         nc.sync.dma_start(
             out=bias_rows[0:HEADS, :], in_=bq.rearrange("(h d) -> h d", d=HEAD)[:, NOPE:HEAD]
         )

@@ -153,7 +153,7 @@ def tile_gptossmlaattention_pb_s_kernel(
         nc.scalar.copy(out=tables_t[:, 1, :], in_=tables_ps[:, 1, :])
 
         rope_q = {}
-        for heads in ((0,), (4,), (1, 2), (3, 5), (6, 7)):
+        for heads in ((0,), (4,), (1, 5), (3, 6), (2, 7)):
             bank = q_banks.tile([P, 2, SEQ], F32, tag="q", name="rope_q")
             for i, h in enumerate(heads):
                 rope_q[h] = bank[:, i, :]
@@ -186,7 +186,7 @@ def tile_gptossmlaattention_pb_s_kernel(
         for h in (0, 4):
             rope_pass(h)
         nope_q = [nope_pass(t) for t in range(T)]
-        for h in (1, 5, 3, 2, 6, 7):
+        for h in (1, 5):
             rope_pass(h)
 
         o_sb = keep.tile([P, HEADS, T, HEAD], F32)
@@ -240,14 +240,18 @@ def tile_gptossmlaattention_pb_s_kernel(
             copy_out(out=o_sb[:, h, done, NOPE:HEAD], in_=rope_ps[:, done, :])
             nc.sync.dma_start(out=out_v[:, h, done, :], in_=o_sb[:, h, done, :])
 
-        for h in GPSIMD_SETS:
+        for h in (0, 1):
             gpsimd_products(h)
         vector_products(4, (0, 1))
         for t in range(T):
             nc.vector.tensor_tensor(
                 out=o_sb[:, :, t, 0:NOPE], in0=nope_q[t][:], in1=nope_bias[:], op=ADD
             )
+        rope_back(*BACK_ORDER[0], nc.scalar.copy)
+        for h in (3, 6, 2, 7):
+            rope_pass(h)
+        gpsimd_products(2)
         for h, sets in ((5, (0, 1)), (3, (0, 1)), (6, (0, 1)), (2, (1,)), (7, (0,)), (7, (1,))):
             vector_products(h, sets)
-        for h, sets in BACK_ORDER:
+        for h, sets in BACK_ORDER[1:]:
             rope_back(h, sets, nc.vector.tensor_copy if (h, sets) == BACK_ORDER[-1] else nc.scalar.copy)

@@ -25,7 +25,7 @@ HEAD = NOPE + ROPE
 N_OUT = HEADS * HEAD
 T = SEQ // P
 GPSIMD_SETS = {0: (0, 1), 1: (0, 1), 2: (0,)}
-IDLE_N = 224
+IDLE_REPS = 3
 BACK_ORDER = (
     (4, (0, 1)), (0, (0, 1)), (5, (0, 1)), (3, (0, 1)), (1, (0, 1)), (6, (0, 1)), (2, (0, 1)),
     (7, (0,)), (7, (1,)),
@@ -45,13 +45,16 @@ def tile_gptossmlaattention_pb_s_kernel(
         o_banks = ctx.enter_context(tc.psum_pool(name="o_banks", bufs=3))
         ctx.enter_context(tc.manual_schedule())
 
-        zeros = keep.tile([P, IDLE_N], F32)
+        zeros = keep.tile([P, P], F32)
         nc.gpsimd.memset(zeros[:], 0.0)
-        idle_ps = q_banks.tile([P, IDLE_N], F32, tag="q")
-        for rep in range(2):
-            nc.tensor.matmul(
-                out=idle_ps[:], lhsT=zeros[:, 0:P], rhs=zeros[:], start=True, stop=True
-            )
+        idle_ps = q_banks.tile([P, IDLE_REPS, P], F32, tag="q")
+        nc.tensor.matmul(
+            out=idle_ps[:],
+            lhsT=zeros[:],
+            rhs=zeros[:].unsqueeze(1).to_broadcast([P, IDLE_REPS, P]),
+            start=True,
+            stop=True,
+        )
 
         biases = keep.tile([P, HEADS * NOPE + P], BF16)
         nc.vector.memset(biases[:].bitcast(I32), 0)

@@ -68,14 +68,16 @@ def tile_gptossmlaattention_pb_s_kernel(
         nc.vector.memset(warm[:], 0.0)
 
         nc.scalar.activation(out=warm[:], in_=warm[:], func=IDENTITY)
-        x_sb = keep.tile([P, T, HID], BF16)
-        nc.sync.dma_start(
-            out=x_sb[:], in_=hidden_states.rearrange("b (p t) k -> p (b t) k", t=T)
-        )
         cos_sb = keep.tile([P, T, ROPE], BF16)
         nc.sync.dma_start(out=cos_sb[:], in_=cos.rearrange("b (p t) j -> p (b t) j", t=T))
         sin_sb = keep.tile([P, T, ROPE], BF16)
         nc.sync.dma_start(out=sin_sb[:], in_=sin.rearrange("b (p t) j -> p (b t) j", t=T))
+        x_sb = keep.tile([P, T, HID], BF16)
+        for t in range(T):
+            nc.sync.dma_start(
+                out=x_sb[:, t, :],
+                in_=hidden_states.rearrange("b (p t) k -> p (b t) k", t=T)[:, t, :],
+            )
         nc.sync.dma_start(
             out=bias_rows[0:HEADS, :], in_=bq.rearrange("(h d) -> h d", d=HEAD)[:, NOPE:HEAD]
         )
@@ -96,7 +98,7 @@ def tile_gptossmlaattention_pb_s_kernel(
         ident = eye[:, HALF : HALF + P]
         exchange = eye[:, 0:P]
         ident_bf = keep.tile([P, P], BF16)
-        make_identity(nc, ident_bf[:])
+        nc.vector.tensor_copy(out=ident_bf[:], in_=ident)
         nc.gpsimd.tensor_copy(out=eye[:, 0:HALF], in_=eye[:, P : P + HALF])
 
         x_words = x_sb[:].bitcast(F32)
@@ -113,6 +115,9 @@ def tile_gptossmlaattention_pb_s_kernel(
                 in_=xt_ps[:].rearrange("p u c -> p c u"),
             )
 
+        tables_ps = o_banks.tile([P, 2, SEQ], BF16, tag="o")
+        for t in range(T):
+            nc.tensor.transpose(tables_ps[:, 0, t * P : (t + 1) * P], cos_sb[:, t, :], ident_bf[:])
         bias_ps = q_banks.tile([P, HEADS], F32, tag="q")
         nc.tensor.matmul(
             out=bias_ps[:], lhsT=bias_rows, rhs=ident_bf[:, 0:HEADS], start=True, stop=True
@@ -127,6 +132,12 @@ def tile_gptossmlaattention_pb_s_kernel(
         nc.vector.tensor_scalar(
             out=sin_x[:, :, HALF:ROPE], in0=sin_sb[:, :, 0:HALF], scalar1=-1.0, scalar2=None, op0=MULT
         )
+        for t in range(T):
+            nc.tensor.transpose(tables_ps[:, 1, t * P : (t + 1) * P], sin_x[:, t, :], ident_bf[:])
+        tables_t = keep.tile([P, 2, SEQ], BF16)
+        nc.scalar.copy(out=tables_t[:, 0, :], in_=tables_ps[:, 0, :])
+        nc.scalar.copy(out=tables_t[:, 1, :], in_=tables_ps[:, 1, :])
+
         for t in range(T):
             cols = slice(t * P, (t + 1) * P)
             nc.vector.quantize_mx(
@@ -146,14 +157,6 @@ def tile_gptossmlaattention_pb_s_kernel(
         nope_bias = keep.tile([P, HEADS, NOPE], F32)
         nc.vector.tensor_copy(out=nope_bias[:].rearrange("p h j -> p (h j)"), in_=spread_ps[:])
 
-        tables_ps = o_banks.tile([P, 2, SEQ], BF16, tag="o")
-        for t in range(T):
-            nc.tensor.transpose(tables_ps[:, 0, t * P : (t + 1) * P], cos_sb[:, t, :], ident_bf[:])
-        for t in range(T):
-            nc.tensor.transpose(tables_ps[:, 1, t * P : (t + 1) * P], sin_x[:, t, :], ident_bf[:])
-        tables_t = keep.tile([P, 2, SEQ], BF16)
-        nc.scalar.copy(out=tables_t[:, 0, :], in_=tables_ps[:, 0, :])
-        nc.scalar.copy(out=tables_t[:, 1, :], in_=tables_ps[:, 1, :])
 
         rope_q = {}
         for heads in ((0,), (4,), (1, 5), (3, 6), (2, 7)):

from contextlib import ExitStack

import concourse.mybir as mybir
from concourse.masks import make_identity

F32 = mybir.dt.float32
BF16 = mybir.dt.bfloat16
I32 = mybir.dt.int32
U8 = mybir.dt.uint8
U32 = mybir.dt.uint32
FP8X4 = mybir.dt.float8_e4m3fn_x4
FP4X4 = mybir.dt.float4_e2m1fn_x4
ADD = mybir.AluOpType.add
MULT = mybir.AluOpType.mult
IDENTITY = mybir.ActivationFunctionType.Identity

P = 128
SEQ = 256
HID = 512
HEADS = 8
NOPE = 64
ROPE = 128
HALF = ROPE // 2
HEAD = NOPE + ROPE
N_OUT = HEADS * HEAD
T = SEQ // P
GPSIMD_SETS = {0: (0, 1), 1: (0, 1), 2: (0,)}
IDLE_REPS = 3
BACK_ORDER = (
    (4, (0, 1)), (0, (0, 1)), (5, (0, 1)), (3, (0, 1)), (1, (0, 1)), (6, (0, 1)), (2, (0, 1)),
    (7, (0,)), (7, (1,)),
)

FLOPS = 2 * SEQ * HID * N_OUT


def tile_gptossmlaattention_pb_s_kernel(
    tc, hidden_states, cos, sin, Wq_words, Wq_scales, bq, out
):
    nc = tc.nc
    with ExitStack() as ctx:
        keep = ctx.enter_context(tc.tile_pool(name="keep", bufs=1))
        per_head = ctx.enter_context(tc.tile_pool(name="per_head", bufs=HEADS))
        q_banks = ctx.enter_context(tc.psum_pool(name="q_banks", bufs=5))
        o_banks = ctx.enter_context(tc.psum_pool(name="o_banks", bufs=3))
        ctx.enter_context(tc.manual_schedule())

        zeros = keep.tile([P, P], F32)
        nc.gpsimd.memset(zeros[:], 0.0)
        idle_ps = q_banks.tile([P, IDLE_REPS, P], F32, tag="q")
        nc.tensor.matmul(
            out=idle_ps[:],
            lhsT=zeros[:],
            rhs=zeros[:].unsqueeze(1).to_broadcast([P, IDLE_REPS, P]),
            start=True,
            stop=True,
        )

        biases = keep.tile([P, HEADS * NOPE + P], BF16)
        nc.vector.memset(biases[:].bitcast(I32), 0)
        nope_bias_row = biases[:, 0 : HEADS * NOPE]
        bias_rows = biases[:, HEADS * NOPE : HEADS * NOPE + P]
        w_scales = keep.tile([P, N_OUT], U8, align_bytes=64)
        nc.vector.memset(w_scales[:].bitcast(I32), 0)
        ones = keep.tile([P, P], BF16)
        nc.vector.memset(ones[:], 1.0)
        warm = keep.tile([P, 1], F32)
        nc.vector.memset(warm[:], 0.0)

        nc.scalar.activation(out=warm[:], in_=warm[:], func=IDENTITY)
        cos_sb = keep.tile([P, T, ROPE], BF16)
        nc.sync.dma_start(out=cos_sb[:], in_=cos.rearrange("b (p t) j -> p (b t) j", t=T))
        sin_sb = keep.tile([P, T, ROPE], BF16)
        nc.sync.dma_start(out=sin_sb[:], in_=sin.rearrange("b (p t) j -> p (b t) j", t=T))
        x_sb = keep.tile([P, T, HID], BF16)
        for t in range(T):
            nc.sync.dma_start(
                out=x_sb[:, t, :],
                in_=hidden_states.rearrange("b (p t) k -> p (b t) k", t=T)[:, t, :],
            )
        nc.sync.dma_start(
            out=bias_rows[0:HEADS, :], in_=bq.rearrange("(h d) -> h d", d=HEAD)[:, NOPE:HEAD]
        )
        nc.sync.dma_start(
            out=nope_bias_row[0:1, :].rearrange("o (h j) -> o h j", h=HEADS),
            in_=bq.rearrange("(o h d) -> o h d", o=1, d=HEAD)[:, :, 0:NOPE],
        )
        w_words = keep.tile([P, 2 * N_OUT], U8, align_bytes=64)
        nc.sync.dma_start(out=w_words[:].bitcast(I32), in_=Wq_words[0].bitcast(I32))
        for quad in range(4):
            nc.sync.dma_start(
                out=w_scales[32 * quad : 32 * quad + 4, :].bitcast(I32),
                in_=Wq_scales[0, 4 * quad : 4 * quad + 4, :].bitcast(I32),
            )

        eye = keep.tile([P, HALF + P], F32)
        make_identity(nc, eye[:, HALF : HALF + P])
        ident = eye[:, HALF : HALF + P]
        exchange = eye[:, 0:P]
        ident_bf = keep.tile([P, P], BF16)
        nc.vector.tensor_copy(out=ident_bf[:], in_=ident)
        nc.gpsimd.tensor_copy(out=eye[:, 0:HALF], in_=eye[:, P : P + HALF])

        x_words = x_sb[:].bitcast(F32)
        x_grouped = keep.tile([P, T, 4 * P], BF16, align_bytes=64)
        x_codes = keep.tile([P, SEQ], U32, align_bytes=64)
        x_scales = keep.tile([P, SEQ], U8, align_bytes=64)
        for t in range(T):
            xt_ps = o_banks.tile([P, 2, P], F32, tag="o", name="xt_ps")
            for u in range(2):
                nc.tensor.transpose(xt_ps[:, u, :], x_words[:, t, u : HID // 2 : 2], ident)
            copy_out = nc.vector.tensor_copy if t == 0 else nc.scalar.copy
            copy_out(
                out=x_grouped[:, t, :].bitcast(F32).rearrange("p (c u) -> p c u", u=2),
                in_=xt_ps[:].rearrange("p u c -> p c u"),
            )

        tables_ps = o_banks.tile([P, 2, SEQ], BF16, tag="o")
        for t in range(T):
            nc.tensor.transpose(tables_ps[:, 0, t * P : (t + 1) * P], cos_sb[:, t, :], ident_bf[:])
        bias_ps = q_banks.tile([P, HEADS], F32, tag="q")
        nc.tensor.matmul(
            out=bias_ps[:], lhsT=bias_rows, rhs=ident_bf[:, 0:HEADS], start=True, stop=True
        )
        bias_t = keep.tile([P, HEADS], F32)
        nc.scalar.copy(out=bias_t[:], in_=bias_ps[:])
        spread_ps = q_banks.tile([P, HEADS * NOPE], F32, tag="q")
        nc.tensor.matmul(out=spread_ps[:], lhsT=ones[:], rhs=nope_bias_row, start=True, stop=True)

        sin_x = keep.tile([P, T, ROPE], BF16)
        nc.vector.tensor_copy(out=sin_x[:, :, 0:HALF], in_=sin_sb[:, :, HALF:ROPE])
        nc.vector.tensor_scalar(
            out=sin_x[:, :, HALF:ROPE], in0=sin_sb[:, :, 0:HALF], scalar1=-1.0, scalar2=None, op0=MULT
        )
        for t in range(T):
            nc.tensor.transpose(tables_ps[:, 1, t * P : (t + 1) * P], sin_x[:, t, :], ident_bf[:])
        tables_t = keep.tile([P, 2, SEQ], BF16)
        nc.scalar.copy(out=tables_t[:, 0, :], in_=tables_ps[:, 0, :])
        nc.scalar.copy(out=tables_t[:, 1, :], in_=tables_ps[:, 1, :])

        for t in range(T):
            cols = slice(t * P, (t + 1) * P)
            nc.vector.quantize_mx(
                out=x_codes[:, cols].bitcast(FP8X4), scales=x_scales[:, cols], in_=x_grouped[:, t, :]
            )
        nope_words = keep.tile([P, 2 * HEADS * NOPE], U8, align_bytes=64)
        nc.vector.tensor_copy(
            out=nope_words[:].bitcast(I32).rearrange("p (h w) -> p h w", h=HEADS),
            in_=w_words[:].bitcast(I32).rearrange("p (h w) -> p h w", h=HEADS)[:, :, 0 : NOPE // 2],
        )
        nope_scales = keep.tile([P, HEADS * NOPE], U8, align_bytes=64)
        nc.vector.tensor_copy(
            out=nope_scales[:].bitcast(I32).rearrange("p (h w) -> p h w", h=HEADS),
            in_=w_scales[:].bitcast(I32).rearrange("p (h w) -> p h w", h=HEADS)[:, :, 0 : NOPE // 4],
        )

        nope_bias = keep.tile([P, HEADS, NOPE], F32)
        nc.vector.tensor_copy(out=nope_bias[:].rearrange("p h j -> p (h j)"), in_=spread_ps[:])


        rope_q = {}
        for heads in ((0,), (4,), (1, 5), (3, 6), (2, 7)):
            bank = q_banks.tile([P, 2, SEQ], F32, tag="q", name="rope_q")
            for i, h in enumerate(heads):
                rope_q[h] = bank[:, i, :]

        def rope_pass(h):
            lo = h * HEAD + NOPE
            nc.tensor.matmul_mx(
                out=rope_q[h],
                lhsT=w_words[:, 2 * lo : 2 * (lo + P)].bitcast(FP4X4),
                lhsT_scale=w_scales[:, lo : lo + P],
                rhs=x_codes[:].bitcast(FP8X4),
                rhs_scale=x_scales[:],
                start=True,
                stop=True,
            )

        def nope_pass(t):
            bank = o_banks.tile([P, HEADS, NOPE], F32, tag="o", name="nope_q")
            nc.tensor.matmul_mx(
                out=bank[:].rearrange("p h j -> p (h j)"),
                lhsT=x_codes[:, t * P : (t + 1) * P].bitcast(FP8X4),
                lhsT_scale=x_scales[:, t * P : (t + 1) * P],
                rhs=nope_words[:].bitcast(FP4X4),
                rhs_scale=nope_scales[:],
                start=True,
                stop=True,
            )
            return bank

        for h in (0, 4):
            rope_pass(h)
        nope_q = [nope_pass(t) for t in range(T)]
        for h in (1, 5):
            rope_pass(h)

        o_sb = keep.tile([P, HEADS, T, HEAD], F32)
        out_v = out.rearrange("b h (p t) d -> p (b h) t d", t=T)
        products = {
            h: per_head.tile([P, 2, SEQ], F32, tag="products", name="products") for h in range(HEADS)
        }

        def gpsimd_products(h):
            width = len(GPSIMD_SETS[h]) * P
            y_sb = per_head.tile([P, SEQ], F32, name="y_sb")
            nc.scalar.activation(
                out=y_sb[:, 0:width],
                in_=rope_q[h][:, 0:width],
                func=IDENTITY,
                bias=bias_t[:, h : h + 1],
                scale=1.0,
            )
            nc.gpsimd.tensor_tensor(
                out=products[h][:, :, 0:width],
                in0=y_sb[:, 0:width].unsqueeze(1).to_broadcast([P, 2, width]),
                in1=tables_t[:, :, 0:width],
                op=MULT,
            )

        def vector_products(h, sets):
            cols = slice(sets[0] * P, (sets[-1] + 1) * P)
            width = len(sets) * P
            nc.vector.scalar_tensor_tensor(
                out=products[h][:, :, cols],
                in0=rope_q[h][:, cols].unsqueeze(1).to_broadcast([P, 2, width]),
                scalar=bias_t[:, h : h + 1],
                in1=tables_t[:, :, cols],
                op0=ADD,
                op1=MULT,
            )

        def rope_back(h, sets, copy_out):
            rope_ps = o_banks.tile([P, T, P], F32, tag="o", name="rope_ps")
            for t in sets:
                rows = slice(t * P, (t + 1) * P)
                nc.tensor.matmul(
                    out=rope_ps[:, t, :], lhsT=products[h][:, 0, rows], rhs=ident,
                    start=True, stop=False, is_transpose=True,
                )
                nc.tensor.matmul(
                    out=rope_ps[:, t, :], lhsT=products[h][:, 1, rows], rhs=exchange,
                    start=False, stop=True, is_transpose=True,
                )
            done = slice(sets[0], sets[-1] + 1)
            copy_out(out=o_sb[:, h, done, NOPE:HEAD], in_=rope_ps[:, done, :])
            nc.sync.dma_start(out=out_v[:, h, done, :], in_=o_sb[:, h, done, :])

        for h in (0, 1):
            gpsimd_products(h)
        vector_products(4, (0, 1))
        for t in range(T):
            nc.vector.tensor_tensor(
                out=o_sb[:, :, t, 0:NOPE], in0=nope_q[t][:], in1=nope_bias[:], op=ADD
            )
        rope_back(*BACK_ORDER[0], nc.scalar.copy)
        for h in (3, 6, 2, 7):
            rope_pass(h)
        gpsimd_products(2)
        for h, sets in ((5, (0, 1)), (3, (0, 1)), (6, (0, 1)), (2, (1,)), (7, (0,)), (7, (1,))):
            vector_products(h, sets)
        for h, sets in BACK_ORDER[1:]:
            rope_back(h, sets, nc.vector.tensor_copy if (h, sets) == BACK_ORDER[-1] else nc.scalar.copy)
